import numpy as np
import ml_dtypes


def mxq(x, axis, fmt="e4m3"):
    dtype, down = {"e4m3": (ml_dtypes.float8_e4m3fn, 7), "e5m2": (ml_dtypes.float8_e5m2, 14)}[fmt]
    v = np.moveaxis(np.asarray(x, np.float32).astype(ml_dtypes.bfloat16).astype(np.float64), axis, -1)
    blocks = v.reshape(v.shape[:-1] + (-1, 32))
    amax = np.abs(blocks).max(-1, keepdims=True)
    byte = np.maximum(np.where(amax > 0, np.frexp(amax)[1] - 1 + 127, 0) - down, 1)
    scale = np.exp2(byte - 127.0)
    codes = (blocks / scale).astype(np.float32).astype(dtype).astype(np.float64)
    return np.moveaxis((codes * scale).reshape(v.shape), -1, axis)


WIDE = False


def mx_kscale(k):
    if not WIDE:
        return np.ones(k)
    levels = np.array([10, -10, 5, -5, 0])
    a = np.random.permutation(np.resize(levels, k // 512 * 4)).reshape(k // 512, 4)
    idx = np.arange(k)
    return np.exp2(a[idx // 512, idx % 128 // 32])


BF16 = ml_dtypes.bfloat16


def bf(x):
    return np.asarray(x, np.float32).astype(BF16)


def f64(x):
    return np.asarray(x).astype(np.float64)


B, S, D_IN, D_OUT, RANK = 4, 2048, 512, 256, 128
ALPHA = 1.0


def setup_inputs():
    s = mx_kscale(D_IN)
    ca = 0.9 * (RANK / D_IN) ** 0.25
    cb = 0.9 * RANK ** 0.25
    return {"x": bf(np.random.standard_normal((B, S, D_IN)) * s),
            "W": bf(np.random.standard_normal((D_IN, D_OUT)) / np.sqrt(D_IN) / s[:, None]),
            "bias": bf(np.random.standard_normal(D_OUT) * 0.5),
            "a0": bf(np.random.standard_normal((D_IN, RANK)) * ca / s[:, None]),
            "b0": bf(np.random.standard_normal((RANK, D_OUT)) * cb),
            "a1": bf(np.random.standard_normal((D_IN, RANK)) * ca),
            "b1": bf(np.random.standard_normal((RANK, D_OUT)) * cb)}


def reference(x, W, bias, a0, b0, a1, b1):
    scale = ALPHA / RANK
    p0 = scale * (f64(a0) @ f64(b0))
    p1 = scale * (f64(a1) @ f64(b1))
    kernel = f64(W) + p0 * p1
    return (mxq(f64(x), 2, "e4m3") @ mxq(kernel, 0, "e4m3")) + f64(bias)

@@ -1,0 +1,199 @@
+from contextlib import ExitStack
+
+import concourse.masks as masks
+import concourse.mybir as mybir
+
+F32 = mybir.dt.float32
+BF16 = mybir.dt.bfloat16
+U32 = mybir.dt.uint32
+U8 = mybir.dt.uint8
+FP8X4 = mybir.dt.float8_e4m3fn_x4
+ADD = mybir.AluOpType.add
+MULT = mybir.AluOpType.mult
+
+P = 128
+TOKENS = 8192
+D_IN = 512
+D_OUT = 256
+RANK = 128
+TILES = TOKENS // P
+GT = 4
+GROUPS = TILES // GT
+WORDS = D_IN // 2
+LOAD_CHUNKS = [4, 4, 8, 16, 16, 16]
+STORE_CHUNKS = [16, 16, 16, 8, 4, 4]
+
+FLOPS = 2 * TOKENS * D_IN * D_OUT + 2 * (2 * D_IN * RANK * D_OUT)
+
+
+def tile_lohawrapper_t_kernel(tc, x, W, bias, a0, b0, a1, b1, out):
+    nc = tc.nc
+    xv = x.flatten_outer_dims().rearrange("(p t) k -> p t k", t=TILES)
+    ov = out.flatten_outer_dims().rearrange("(p t) n -> p t n", t=TILES)
+    with ExitStack() as ctx:
+        keep = ctx.enter_context(tc.tile_pool(name="keep", bufs=1))
+        stage = ctx.enter_context(tc.tile_pool(name="stage", bufs=4))
+        psum = ctx.enter_context(tc.psum_pool(name="psum", bufs=1))
+        ctx.enter_context(tc.manual_schedule())
+
+        ident_bf = keep.tile([P, P], BF16, name="ident_bf")
+        masks.make_identity(nc, ident_bf[:])
+        ident_f = keep.tile([P, P], F32, name="ident_f")
+        masks.make_identity(nc, ident_f[:])
+        bias_row = keep.tile([P, D_OUT], BF16, name="bias_row")
+        nc.vector.memset(bias_row[:], 0.0)
+        ones = keep.tile([P, P], BF16, name="ones")
+        nc.vector.memset(ones[:], 1.0)
+
+        a_sb = []
+        for i, a in enumerate((a0, a1)):
+            t = keep.tile([P, 4 * RANK], BF16, name="a%d_sb" % i)
+            nc.sync.dma_start(
+                out=t[:].rearrange("p (u c) -> p u c", u=2),
+                in_=a.rearrange("(u p e) r -> p u (e r)", u=2, e=2),
+            )
+            a_sb.append(t)
+        b_sb = []
+        for i, b in enumerate((b0, b1)):
+            t = keep.tile([P, D_OUT], BF16, name="b%d_sb" % i)
+            nc.sync.dma_start(out=t[:], in_=b)
+            b_sb.append(t)
+        x_sb = []
+        w_sb = keep.tile([P, 4 * D_OUT], BF16, name="w_sb")
+        t0 = 0
+        for c, n in enumerate(LOAD_CHUNKS):
+            t = keep.tile([P, n * D_IN], BF16, name="x%d" % c)
+            nc.sync.dma_start(out=t[:].rearrange("p (t k) -> p t k", k=D_IN), in_=xv[:, t0 : t0 + n, :])
+            for i in range(n):
+                x_sb.append((t, i))
+            t0 += n
+            if c == 0:
+                nc.sync.dma_start(
+                    out=w_sb[:].rearrange("p (u c) -> p u c", u=2),
+                    in_=W.rearrange("(u p e) n -> p u (e n)", u=2, e=2),
+                )
+                nc.sync.dma_start(out=bias_row[0:1, :], in_=bias.rearrange("(o n) -> o n", o=1))
+
+        b0s = keep.tile([P, D_OUT], BF16, name="b0s")
+        nc.vector.tensor_scalar_mul(out=b0s[:], in0=b_sb[0][:], scalar1=1.0 / (RANK * RANK))
+        rhs_b = [b0s, b_sb[1]]
+        aT = []
+        for i in range(2):
+            ps = psum.tile([P, 4 * P], BF16, name="aT_ps%d" % i, tag="mm%d" % i)
+            for t in range(4):
+                nc.tensor.transpose(ps[:, t * P : (t + 1) * P], a_sb[i][:, t * P : (t + 1) * P], ident_bf[:])
+            sb = keep.tile([P, 4 * P], BF16, name="aT%d" % i)
+            nc.vector.tensor_copy(out=sb[:], in_=ps[:])
+            aT.append(sb)
+        p0s = keep.tile([P, 4 * D_OUT], F32, name="p0s")
+        prod = keep.tile([P, 4 * D_OUT], F32, name="prod")
+        for i in range(2):
+            for j in range(2):
+                ps = psum.tile([P, 2 * D_OUT], F32, name="p%d_ps%d" % (i, j), tag="mm%d" % ((2 + 2 * i + j) % 4))
+                for h in range(2):
+                    t = 2 * j + h
+                    nc.tensor.matmul(
+                        out=ps[:, h * D_OUT : (h + 1) * D_OUT],
+                        lhsT=aT[i][:, t * P : (t + 1) * P],
+                        rhs=rhs_b[i][:],
+                        start=True,
+                        stop=True,
+                    )
+                cols = slice(j * 2 * D_OUT, (j + 1) * 2 * D_OUT)
+                if i == 0:
+                    nc.scalar.copy(out=p0s[:, cols], in_=ps[:])
+                else:
+                    nc.vector.tensor_tensor(out=prod[:, cols], in0=ps[:], in1=p0s[:, cols], op=MULT)
+        bias_ps = psum.tile([P, D_OUT], F32, name="bias_ps", tag="tr3")
+        nc.tensor.matmul(out=bias_ps[:], lhsT=ones[:], rhs=bias_row[:], start=True, stop=True)
+        bias2 = keep.tile([P, 2 * D_OUT], F32, name="bias2")
+        for h in range(2):
+            nc.scalar.copy(out=bias2[:, h * D_OUT : (h + 1) * D_OUT], in_=bias_ps[:])
+        kern_g = keep.tile([P, 4 * D_OUT], BF16, name="kern_g", align_bytes=64)
+        nc.vector.tensor_tensor(
+            out=kern_g[:].rearrange("p (n t) -> p n t", t=4),
+            in0=prod[:].rearrange("p (t n) -> p n t", t=4),
+            in1=w_sb[:].rearrange("p (t n) -> p n t", t=4),
+            op=ADD,
+        )
+        k_codes = keep.tile([P, D_OUT], U32, name="k_codes", align_bytes=64)
+        k_scales = keep.tile([P, D_OUT], U8, name="k_scales", align_bytes=64)
+        nc.vector.quantize_mx(out=k_codes[:].bitcast(FP8X4), scales=k_scales[:], in_=kern_g[:])
+
+        grouped = {}
+        codes = {}
+        scales = {}
+        acc = {}
+        o_sb = []
+        for c, n in enumerate(STORE_CHUNKS):
+            t = keep.tile([P, n * D_OUT], F32, name="o%d" % c)
+            for i in range(n):
+                o_sb.append((c, t, i, n))
+
+        def transposes_and_copies(g):
+            gr = stage.tile([P, GT * D_IN], BF16, name="grouped%d" % g, tag="grouped", align_bytes=64)
+            gr_words = gr[:].bitcast(F32)
+            for b in range(2):
+                ps = psum.tile([P, 4 * P], F32, name="tr%d_%d" % (g, b), tag="tr%d" % ((2 * g + b) % 4))
+                for j in range(2):
+                    xt, i = x_sb[GT * g + 2 * b + j]
+                    words = xt[:].bitcast(F32)
+                    for u in range(2):
+                        s = 2 * j + u
+                        nc.tensor.transpose(
+                            ps[:, s * P : (s + 1) * P],
+                            words[:, i * WORDS + u * P : i * WORDS + (u + 1) * P],
+                            ident_f[:],
+                        )
+                nc.scalar.copy(
+                    out=gr_words[:, b * 4 * P : (b + 1) * 4 * P].rearrange("p (j r u) -> p j r u", j=2, u=2),
+                    in_=ps[:].rearrange("p (j u r) -> p j r u", j=2, u=2),
+                )
+            grouped[g] = gr
+
+        def quantise(g):
+            codes[g] = keep.tile([P, GT * P], U32, name="codes%d" % g, align_bytes=64)
+            scales[g] = keep.tile([P, GT * P], U8, name="scales%d" % g, align_bytes=64)
+            nc.vector.quantize_mx(out=codes[g][:].bitcast(FP8X4), scales=scales[g][:], in_=grouped[g][:])
+
+        def multiply(g):
+            acc[g] = []
+            for b in range(2):
+                ps = psum.tile([P, 2 * D_OUT], F32, name="mm%d_%d" % (g, b), tag="mm%d" % ((2 * g + b) % 4))
+                for j in range(2):
+                    cols = slice((2 * b + j) * P, (2 * b + j + 1) * P)
+                    nc.tensor.matmul_mx(
+                        out=ps[:, j * D_OUT : (j + 1) * D_OUT],
+                        lhsT=codes[g][:, cols].bitcast(FP8X4),
+                        lhsT_scale=scales[g][:, cols],
+                        rhs=k_codes[:].bitcast(FP8X4),
+                        rhs_scale=k_scales[:],
+                        start=True,
+                        stop=True,
+                    )
+                acc[g].append(ps)
+
+        def add_bias_and_store(g):
+            for b in range(2):
+                tile_no = GT * g + 2 * b
+                c, t, i, n = o_sb[tile_no]
+                nc.vector.tensor_tensor(
+                    out=t[:, i * D_OUT : (i + 2) * D_OUT], in0=acc[g][b][:], in1=bias2[:], op=ADD
+                )
+                if i + 2 == n:
+                    first = tile_no + 2 - n
+                    nc.sync.dma_start(
+                        out=ov[:, first : first + n, :], in_=t[:].rearrange("p (t n) -> p t n", n=D_OUT)
+                    )
+
+        for g in range(3):
+            transposes_and_copies(g)
+        for g in range(2):
+            quantise(g)
+        for g in range(GROUPS):
+            multiply(g)
+            if g + 3 < GROUPS:
+                transposes_and_copies(g + 3)
+            add_bias_and_store(g)
+            if g + 2 < GROUPS:
+                quantise(g + 2)

@@ -21,7 +21,8 @@ GT = 4
 GROUPS = TILES // GT
 WORDS = D_IN // 2
 LOAD_CHUNKS = [4, 4, 8, 16, 16, 16]
-STORE_CHUNKS = [16, 16, 16, 8, 4, 4]
+STORE_CHUNKS = [16, 8, 8, 8, 8, 8, 4, 4]
+OFFLOAD = (0, 2, 4, 6, 8, 10, 12, 14)
 
 FLOPS = 2 * TOKENS * D_IN * D_OUT + 2 * (2 * D_IN * RANK * D_OUT)
 
@@ -173,13 +174,19 @@ def tile_lohawrapper_t_kernel(tc, x, W, bias, a0, b0, a1, b1, out):
                     )
                 acc[g].append(ps)
 
+        def copy_out(g):
+            c, t, i, n = o_sb[GT * g]
+            nc.scalar.copy(out=t[:, i * D_OUT : (i + 2) * D_OUT], in_=acc[g][0][:])
+
         def add_bias_and_store(g):
             for b in range(2):
                 tile_no = GT * g + 2 * b
                 c, t, i, n = o_sb[tile_no]
-                nc.vector.tensor_tensor(
-                    out=t[:, i * D_OUT : (i + 2) * D_OUT], in0=acc[g][b][:], in1=bias2[:], op=ADD
-                )
+                dst = t[:, i * D_OUT : (i + 2) * D_OUT]
+                if b == 0 and g in OFFLOAD:
+                    nc.gpsimd.tensor_tensor(out=dst, in0=dst, in1=bias2[:], op=ADD)
+                else:
+                    nc.vector.tensor_tensor(out=dst, in0=acc[g][b][:], in1=bias2[:], op=ADD)
                 if i + 2 == n:
                     first = tile_no + 2 - n
                     nc.sync.dma_start(
@@ -192,6 +199,8 @@ def tile_lohawrapper_t_kernel(tc, x, W, bias, a0, b0, a1, b1, out):
             quantise(g)
         for g in range(GROUPS):
             multiply(g)
+            if g in OFFLOAD:
+                copy_out(g)
             if g + 3 < GROUPS:
                 transposes_and_copies(g + 3)
             add_bias_and_store(g)

@@ -21,8 +21,8 @@ GT = 4
 GROUPS = TILES // GT
 WORDS = D_IN // 2
 LOAD_CHUNKS = [4, 4, 8, 16, 16, 16]
-STORE_CHUNKS = [16, 8, 8, 8, 8, 8, 4, 4]
-OFFLOAD = (0, 2, 4, 6, 8, 10, 12, 14)
+STORE_CHUNKS = [16, 16, 16, 8, 4, 2, 2]
+WARM = 4
 
 FLOPS = 2 * TOKENS * D_IN * D_OUT + 2 * (2 * D_IN * RANK * D_OUT)
 
@@ -37,6 +37,11 @@ def tile_lohawrapper_t_kernel(tc, x, W, bias, a0, b0, a1, b1, out):
         psum = ctx.enter_context(tc.psum_pool(name="psum", bufs=1))
         ctx.enter_context(tc.manual_schedule())
 
+        warm = keep.tile([P, 4 * P], BF16, name="warm")
+        nc.vector.memset(warm[:], 0.0)
+        warm_ps = psum.tile([P, 4 * P], F32, name="warm_ps", tag="tr0")
+        for i in range(WARM):
+            nc.tensor.matmul(out=warm_ps[:], lhsT=warm[:, 0:P], rhs=warm[:], start=True, stop=True)
         ident_bf = keep.tile([P, P], BF16, name="ident_bf")
         masks.make_identity(nc, ident_bf[:])
         ident_f = keep.tile([P, P], F32, name="ident_f")
@@ -174,19 +179,13 @@ def tile_lohawrapper_t_kernel(tc, x, W, bias, a0, b0, a1, b1, out):
                     )
                 acc[g].append(ps)
 
-        def copy_out(g):
-            c, t, i, n = o_sb[GT * g]
-            nc.scalar.copy(out=t[:, i * D_OUT : (i + 2) * D_OUT], in_=acc[g][0][:])
-
         def add_bias_and_store(g):
             for b in range(2):
                 tile_no = GT * g + 2 * b
                 c, t, i, n = o_sb[tile_no]
-                dst = t[:, i * D_OUT : (i + 2) * D_OUT]
-                if b == 0 and g in OFFLOAD:
-                    nc.gpsimd.tensor_tensor(out=dst, in0=dst, in1=bias2[:], op=ADD)
-                else:
-                    nc.vector.tensor_tensor(out=dst, in0=acc[g][b][:], in1=bias2[:], op=ADD)
+                nc.vector.tensor_tensor(
+                    out=t[:, i * D_OUT : (i + 2) * D_OUT], in0=acc[g][b][:], in1=bias2[:], op=ADD
+                )
                 if i + 2 == n:
                     first = tile_no + 2 - n
                     nc.sync.dma_start(
@@ -199,8 +198,6 @@ def tile_lohawrapper_t_kernel(tc, x, W, bias, a0, b0, a1, b1, out):
             quantise(g)
         for g in range(GROUPS):
             multiply(g)
-            if g in OFFLOAD:
-                copy_out(g)
             if g + 3 < GROUPS:
                 transposes_and_copies(g + 3)
             add_bias_and_store(g)

@@ -20,9 +20,8 @@ TILES = TOKENS // P
 GT = 4
 GROUPS = TILES // GT
 WORDS = D_IN // 2
-LOAD_CHUNKS = [4, 4, 8, 16, 16, 16]
-STORE_CHUNKS = [16, 16, 16, 8, 4, 2, 2]
-WARM = 4
+LOAD_CHUNKS = [4, 4, 4, 4, 8, 8, 16, 16]
+STORE_CHUNKS = [16, 16, 8, 8, 8, 4, 4]
 
 FLOPS = 2 * TOKENS * D_IN * D_OUT + 2 * (2 * D_IN * RANK * D_OUT)
 
@@ -37,11 +36,6 @@ def tile_lohawrapper_t_kernel(tc, x, W, bias, a0, b0, a1, b1, out):
         psum = ctx.enter_context(tc.psum_pool(name="psum", bufs=1))
         ctx.enter_context(tc.manual_schedule())
 
-        warm = keep.tile([P, 4 * P], BF16, name="warm")
-        nc.vector.memset(warm[:], 0.0)
-        warm_ps = psum.tile([P, 4 * P], F32, name="warm_ps", tag="tr0")
-        for i in range(WARM):
-            nc.tensor.matmul(out=warm_ps[:], lhsT=warm[:, 0:P], rhs=warm[:], start=True, stop=True)
         ident_bf = keep.tile([P, P], BF16, name="ident_bf")
         masks.make_identity(nc, ident_bf[:])
         ident_f = keep.tile([P, P], F32, name="ident_f")
@@ -59,6 +53,7 @@ def tile_lohawrapper_t_kernel(tc, x, W, bias, a0, b0, a1, b1, out):
                 in_=a.rearrange("(u p e) r -> p u (e r)", u=2, e=2),
             )
             a_sb.append(t)
+        nc.sync.dma_start(out=bias_row[0:1, :], in_=bias.rearrange("(o n) -> o n", o=1))
         b_sb = []
         for i, b in enumerate((b0, b1)):
             t = keep.tile([P, D_OUT], BF16, name="b%d_sb" % i)
@@ -78,7 +73,6 @@ def tile_lohawrapper_t_kernel(tc, x, W, bias, a0, b0, a1, b1, out):
                     out=w_sb[:].rearrange("p (u c) -> p u c", u=2),
                     in_=W.rearrange("(u p e) n -> p u (e n)", u=2, e=2),
                 )
-                nc.sync.dma_start(out=bias_row[0:1, :], in_=bias.rearrange("(o n) -> o n", o=1))
 
         b0s = keep.tile([P, D_OUT], BF16, name="b0s")
         nc.vector.tensor_scalar_mul(out=b0s[:], in0=b_sb[0][:], scalar1=1.0 / (RANK * RANK))

from contextlib import ExitStack

import concourse.masks as masks
import concourse.mybir as mybir

F32 = mybir.dt.float32
BF16 = mybir.dt.bfloat16
U32 = mybir.dt.uint32
U8 = mybir.dt.uint8
FP8X4 = mybir.dt.float8_e4m3fn_x4
ADD = mybir.AluOpType.add
MULT = mybir.AluOpType.mult

P = 128
TOKENS = 8192
D_IN = 512
D_OUT = 256
RANK = 128
TILES = TOKENS // P
GT = 4
GROUPS = TILES // GT
WORDS = D_IN // 2
LOAD_CHUNKS = [4, 4, 4, 4, 8, 8, 16, 16]
STORE_CHUNKS = [16, 16, 8, 8, 8, 4, 4]

FLOPS = 2 * TOKENS * D_IN * D_OUT + 2 * (2 * D_IN * RANK * D_OUT)


def tile_lohawrapper_t_kernel(tc, x, W, bias, a0, b0, a1, b1, out):
    nc = tc.nc
    xv = x.flatten_outer_dims().rearrange("(p t) k -> p t k", t=TILES)
    ov = out.flatten_outer_dims().rearrange("(p t) n -> p t n", t=TILES)
    with ExitStack() as ctx:
        keep = ctx.enter_context(tc.tile_pool(name="keep", bufs=1))
        stage = ctx.enter_context(tc.tile_pool(name="stage", bufs=4))
        psum = ctx.enter_context(tc.psum_pool(name="psum", bufs=1))
        ctx.enter_context(tc.manual_schedule())

        ident_bf = keep.tile([P, P], BF16, name="ident_bf")
        masks.make_identity(nc, ident_bf[:])
        ident_f = keep.tile([P, P], F32, name="ident_f")
        masks.make_identity(nc, ident_f[:])
        bias_row = keep.tile([P, D_OUT], BF16, name="bias_row")
        nc.vector.memset(bias_row[:], 0.0)
        ones = keep.tile([P, P], BF16, name="ones")
        nc.vector.memset(ones[:], 1.0)

        a_sb = []
        for i, a in enumerate((a0, a1)):
            t = keep.tile([P, 4 * RANK], BF16, name="a%d_sb" % i)
            nc.sync.dma_start(
                out=t[:].rearrange("p (u c) -> p u c", u=2),
                in_=a.rearrange("(u p e) r -> p u (e r)", u=2, e=2),
            )
            a_sb.append(t)
        nc.sync.dma_start(out=bias_row[0:1, :], in_=bias.rearrange("(o n) -> o n", o=1))
        b_sb = []
        for i, b in enumerate((b0, b1)):
            t = keep.tile([P, D_OUT], BF16, name="b%d_sb" % i)
            nc.sync.dma_start(out=t[:], in_=b)
            b_sb.append(t)
        x_sb = []
        w_sb = keep.tile([P, 4 * D_OUT], BF16, name="w_sb")
        t0 = 0
        for c, n in enumerate(LOAD_CHUNKS):
            t = keep.tile([P, n * D_IN], BF16, name="x%d" % c)
            nc.sync.dma_start(out=t[:].rearrange("p (t k) -> p t k", k=D_IN), in_=xv[:, t0 : t0 + n, :])
            for i in range(n):
                x_sb.append((t, i))
            t0 += n
            if c == 0:
                nc.sync.dma_start(
                    out=w_sb[:].rearrange("p (u c) -> p u c", u=2),
                    in_=W.rearrange("(u p e) n -> p u (e n)", u=2, e=2),
                )

        b0s = keep.tile([P, D_OUT], BF16, name="b0s")
        nc.vector.tensor_scalar_mul(out=b0s[:], in0=b_sb[0][:], scalar1=1.0 / (RANK * RANK))
        rhs_b = [b0s, b_sb[1]]
        aT = []
        for i in range(2):
            ps = psum.tile([P, 4 * P], BF16, name="aT_ps%d" % i, tag="mm%d" % i)
            for t in range(4):
                nc.tensor.transpose(ps[:, t * P : (t + 1) * P], a_sb[i][:, t * P : (t + 1) * P], ident_bf[:])
            sb = keep.tile([P, 4 * P], BF16, name="aT%d" % i)
            nc.vector.tensor_copy(out=sb[:], in_=ps[:])
            aT.append(sb)
        p0s = keep.tile([P, 4 * D_OUT], F32, name="p0s")
        prod = keep.tile([P, 4 * D_OUT], F32, name="prod")
        for i in range(2):
            for j in range(2):
                ps = psum.tile([P, 2 * D_OUT], F32, name="p%d_ps%d" % (i, j), tag="mm%d" % ((2 + 2 * i + j) % 4))
                for h in range(2):
                    t = 2 * j + h
                    nc.tensor.matmul(
                        out=ps[:, h * D_OUT : (h + 1) * D_OUT],
                        lhsT=aT[i][:, t * P : (t + 1) * P],
                        rhs=rhs_b[i][:],
                        start=True,
                        stop=True,
                    )
                cols = slice(j * 2 * D_OUT, (j + 1) * 2 * D_OUT)
                if i == 0:
                    nc.scalar.copy(out=p0s[:, cols], in_=ps[:])
                else:
                    nc.vector.tensor_tensor(out=prod[:, cols], in0=ps[:], in1=p0s[:, cols], op=MULT)
        bias_ps = psum.tile([P, D_OUT], F32, name="bias_ps", tag="tr3")
        nc.tensor.matmul(out=bias_ps[:], lhsT=ones[:], rhs=bias_row[:], start=True, stop=True)
        bias2 = keep.tile([P, 2 * D_OUT], F32, name="bias2")
        for h in range(2):
            nc.scalar.copy(out=bias2[:, h * D_OUT : (h + 1) * D_OUT], in_=bias_ps[:])
        kern_g = keep.tile([P, 4 * D_OUT], BF16, name="kern_g", align_bytes=64)
        nc.vector.tensor_tensor(
            out=kern_g[:].rearrange("p (n t) -> p n t", t=4),
            in0=prod[:].rearrange("p (t n) -> p n t", t=4),
            in1=w_sb[:].rearrange("p (t n) -> p n t", t=4),
            op=ADD,
        )
        k_codes = keep.tile([P, D_OUT], U32, name="k_codes", align_bytes=64)
        k_scales = keep.tile([P, D_OUT], U8, name="k_scales", align_bytes=64)
        nc.vector.quantize_mx(out=k_codes[:].bitcast(FP8X4), scales=k_scales[:], in_=kern_g[:])

        grouped = {}
        codes = {}
        scales = {}
        acc = {}
        o_sb = []
        for c, n in enumerate(STORE_CHUNKS):
            t = keep.tile([P, n * D_OUT], F32, name="o%d" % c)
            for i in range(n):
                o_sb.append((c, t, i, n))

        def transposes_and_copies(g):
            gr = stage.tile([P, GT * D_IN], BF16, name="grouped%d" % g, tag="grouped", align_bytes=64)
            gr_words = gr[:].bitcast(F32)
            for b in range(2):
                ps = psum.tile([P, 4 * P], F32, name="tr%d_%d" % (g, b), tag="tr%d" % ((2 * g + b) % 4))
                for j in range(2):
                    xt, i = x_sb[GT * g + 2 * b + j]
                    words = xt[:].bitcast(F32)
                    for u in range(2):
                        s = 2 * j + u
                        nc.tensor.transpose(
                            ps[:, s * P : (s + 1) * P],
                            words[:, i * WORDS + u * P : i * WORDS + (u + 1) * P],
                            ident_f[:],
                        )
                nc.scalar.copy(
                    out=gr_words[:, b * 4 * P : (b + 1) * 4 * P].rearrange("p (j r u) -> p j r u", j=2, u=2),
                    in_=ps[:].rearrange("p (j u r) -> p j r u", j=2, u=2),
                )
            grouped[g] = gr

        def quantise(g):
            codes[g] = keep.tile([P, GT * P], U32, name="codes%d" % g, align_bytes=64)
            scales[g] = keep.tile([P, GT * P], U8, name="scales%d" % g, align_bytes=64)
            nc.vector.quantize_mx(out=codes[g][:].bitcast(FP8X4), scales=scales[g][:], in_=grouped[g][:])

        def multiply(g):
            acc[g] = []
            for b in range(2):
                ps = psum.tile([P, 2 * D_OUT], F32, name="mm%d_%d" % (g, b), tag="mm%d" % ((2 * g + b) % 4))
                for j in range(2):
                    cols = slice((2 * b + j) * P, (2 * b + j + 1) * P)
                    nc.tensor.matmul_mx(
                        out=ps[:, j * D_OUT : (j + 1) * D_OUT],
                        lhsT=codes[g][:, cols].bitcast(FP8X4),
                        lhsT_scale=scales[g][:, cols],
                        rhs=k_codes[:].bitcast(FP8X4),
                        rhs_scale=k_scales[:],
                        start=True,
                        stop=True,
                    )
                acc[g].append(ps)

        def add_bias_and_store(g):
            for b in range(2):
                tile_no = GT * g + 2 * b
                c, t, i, n = o_sb[tile_no]
                nc.vector.tensor_tensor(
                    out=t[:, i * D_OUT : (i + 2) * D_OUT], in0=acc[g][b][:], in1=bias2[:], op=ADD
                )
                if i + 2 == n:
                    first = tile_no + 2 - n
                    nc.sync.dma_start(
                        out=ov[:, first : first + n, :], in_=t[:].rearrange("p (t n) -> p t n", n=D_OUT)
                    )

        for g in range(3):
            transposes_and_copies(g)
        for g in range(2):
            quantise(g)
        for g in range(GROUPS):
            multiply(g)
            if g + 3 < GROUPS:
                transposes_and_copies(g + 3)
            add_bias_and_store(g)
            if g + 2 < GROUPS:
                quantise(g + 2)
